import numpy as np
import ml_dtypes


def mxq(x, axis, fmt="e4m3"):
    dtype, down = {"e4m3": (ml_dtypes.float8_e4m3fn, 7), "e5m2": (ml_dtypes.float8_e5m2, 14)}[fmt]
    v = np.moveaxis(np.asarray(x, np.float32).astype(ml_dtypes.bfloat16).astype(np.float64), axis, -1)
    blocks = v.reshape(v.shape[:-1] + (-1, 32))
    amax = np.abs(blocks).max(-1, keepdims=True)
    byte = np.maximum(np.where(amax > 0, np.frexp(amax)[1] - 1 + 127, 0) - down, 1)
    scale = np.exp2(byte - 127.0)
    codes = (blocks / scale).astype(np.float32).astype(dtype).astype(np.float64)
    return np.moveaxis((codes * scale).reshape(v.shape), -1, axis)


WIDE = False


def mx_kscale(k):
    if not WIDE:
        return np.ones(k)
    levels = np.array([10, -10, 5, -5, 0])
    a = np.random.permutation(np.resize(levels, k // 512 * 4)).reshape(k // 512, 4)
    idx = np.arange(k)
    return np.exp2(a[idx // 512, idx % 128 // 32])


BF16 = ml_dtypes.bfloat16


def bf(x):
    return np.asarray(x, np.float32).astype(BF16)


def f64(x):
    return np.asarray(x).astype(np.float64)


N, F, D1, D2, D3, D4, D5 = 2048, 64, 16, 1024, 512, 1024, 256
EDGE_PROB = 0.003
ELU_ALPHA = 1.0
DEG = 2.0 * EDGE_PROB * N


def elu(v):
    return np.where(v > 0.0, v, ELU_ALPHA * (np.exp(np.minimum(v, 0.0)) - 1.0))


def adjacency():
    u = np.random.uniform(size=(N, N))
    a = np.where(u < EDGE_PROB, 1.0, 0.0)
    return np.maximum(a, a.T)


def setup_inputs():
    s = mx_kscale(D2)
    return {"t3": bf(np.random.standard_normal((N, D2)) * 0.4 * DEG * s),
            "W2": bf(np.random.standard_normal((D2, D3)) * 0.55 / np.sqrt(D2 * DEG) / s[:, None]),
            "A": bf(adjacency())}


def reference(t3, W2, A):
    a3 = mxq(f64(t3), 1, "e4m3") @ mxq(f64(W2), 0, "e4m3")
    h3 = elu(a3)
    t4 = mxq(f64(A), 1, "e4m3") @ mxq(h3, 0, "e4m3")
    return a3, t4

@@ -1,0 +1,215 @@
+from contextlib import ExitStack
+
+import concourse.mybir as mybir
+from concourse.masks import make_identity
+
+F32 = mybir.dt.float32
+BF16 = mybir.dt.bfloat16
+U32 = mybir.dt.uint32
+U8 = mybir.dt.uint8
+FP8X4 = mybir.dt.float8_e4m3fn_x4
+ALU = mybir.AluOpType
+ACT = mybir.ActivationFunctionType
+
+P = 128
+PACK = 4
+K_PASS = P * PACK
+
+NODES = 2048
+FEATURES = 1024
+WIDTH = 512
+
+FEATURE_PASSES = FEATURES // K_PASS
+NODE_GROUPS = NODES // K_PASS
+
+STAGE_VALUES = 4096
+STAGE_WORDS = STAGE_VALUES // 2
+STAGE_CODES = STAGE_VALUES // PACK
+BANK_WORDS = 512
+STAGE_BANKS = STAGE_WORDS // BANK_WORDS
+T3_STAGES = NODES * FEATURES // (P * STAGE_VALUES)
+A_STAGES = NODES * NODES // (P * STAGE_VALUES)
+STAGES = T3_STAGES + A_STAGES
+A_TILES = STAGE_VALUES // NODES
+
+AHEAD = 2
+RESIDENT = 8
+VECTOR_BANK = 3
+
+FLOPS = 2 * NODES * FEATURES * WIDTH + 2 * NODES * NODES * WIDTH
+
+
+def tile_gcn_kron_pa_kernel(tc, t3, W2, A, out_0, out_1):
+    nc = tc.nc
+
+    t3_stage = t3.rearrange("(g u p e) k -> g p u e k", g=T3_STAGES, u=2, p=P, e=2)
+    a3_stage = out_0.rearrange("(g u p e) d -> g p u e d", g=T3_STAGES, u=2, p=P, e=2)
+    a_stage = A.rearrange("(i p r) m -> i p r m", i=A_STAGES, p=P, r=A_TILES)
+    t4_stage = out_1.rearrange("(i p r) d -> i p r d", i=A_STAGES, p=P, r=A_TILES)
+    w2_pass = W2.rearrange("(c u q e) d -> c q u e d", c=FEATURE_PASSES, u=2, q=P, e=2)
+
+    with ExitStack() as ctx:
+        const = ctx.enter_context(tc.tile_pool(name="const", bufs=1))
+        rows_pool = ctx.enter_context(tc.tile_pool(name="rows", bufs=RESIDENT))
+        grouped_pool = ctx.enter_context(tc.tile_pool(name="grouped", bufs=2))
+        codes_pool = ctx.enter_context(tc.tile_pool(name="codes", bufs=AHEAD + 2))
+        a3_pool = ctx.enter_context(tc.tile_pool(name="a3", bufs=T3_STAGES))
+        elu_pool = ctx.enter_context(tc.tile_pool(name="elu", bufs=2))
+        t4_pool = ctx.enter_context(tc.tile_pool(name="t4", bufs=3))
+        flip_psum = ctx.enter_context(tc.psum_pool(name="flip", bufs=STAGE_BANKS))
+        sum_psum = ctx.enter_context(tc.psum_pool(name="sums", bufs=4))
+        ctx.enter_context(tc.manual_schedule())
+
+        rows_of = {}
+
+        def load_stage(i):
+            rows = rows_pool.tile([P, STAGE_VALUES], BF16)
+            if i < T3_STAGES:
+                nc.sync.dma_start(
+                    out=rows[:].rearrange("p (u e k) -> p u e k", u=2, e=2), in_=t3_stage[i]
+                )
+            else:
+                nc.sync.dma_start(
+                    out=rows[:].rearrange("p (r m) -> p r m", r=A_TILES), in_=a_stage[i - T3_STAGES]
+                )
+            rows_of[i] = rows
+
+        w2_rows = const.tile([P, FEATURE_PASSES, PACK, WIDTH], BF16)
+        for c in range(FEATURE_PASSES):
+            nc.sync.dma_start(
+                out=w2_rows[:, c].rearrange("p (u e) d -> p u e d", e=2), in_=w2_pass[c]
+            )
+        for i in range(RESIDENT):
+            load_stage(i)
+
+        ident = const.tile([P, P], F32)
+        make_identity(nc, ident[:])
+
+        zero = const.tile([P, 1], F32)
+        one = const.tile([P, 1], F32)
+        nc.vector.memset(zero[:], 0.0)
+        nc.scalar.activation(out=one[:], in_=zero[:], func=ACT.Exp)
+
+        w2_grouped = const.tile([P, FEATURE_PASSES, WIDTH, PACK], BF16, align_bytes=64)
+        w2_codes = const.tile([P, FEATURE_PASSES, WIDTH], U32, align_bytes=64)
+        w2_scales = const.tile([P, FEATURE_PASSES, WIDTH], U8, align_bytes=64)
+        for c in range(FEATURE_PASSES):
+            nc.vector.tensor_copy(
+                out=w2_grouped[:, c].rearrange("p (x i) t -> p x t i", i=4),
+                in_=w2_rows[:, c].rearrange("p t (x i) -> p x t i", i=4),
+            )
+        for c in range(FEATURE_PASSES):
+            nc.vector.quantize_mx(
+                out=w2_codes[:, c].bitcast(FP8X4),
+                scales=w2_scales[:, c],
+                in_=w2_grouped[:, c].rearrange("p d t -> p (d t)"),
+            )
+
+        h_codes = const.tile([P, NODE_GROUPS, WIDTH], U32, align_bytes=64)
+        h_scales = const.tile([P, NODE_GROUPS, WIDTH], U8, align_bytes=64)
+
+        def transpose_and_quantise(i):
+            words = rows_of[i][:].bitcast(F32)
+            grouped = grouped_pool.tile([P, STAGE_VALUES], BF16, align_bytes=64)
+            grouped_words = grouped[:].bitcast(F32).rearrange(
+                "p (b o n u) -> p b o n u", b=STAGE_BANKS, o=2, n=P, u=2
+            )
+            codes = codes_pool.tile([P, STAGE_CODES], U32, align_bytes=64)
+            scales = codes_pool.tile([P, STAGE_CODES], U8, align_bytes=64)
+            for b in range(STAGE_BANKS):
+                flipped = flip_psum.tile([P, BANK_WORDS // P, P], F32)
+                for x in range(BANK_WORDS // P):
+                    first = b * BANK_WORDS + x * P
+                    nc.tensor.transpose(flipped[:, x, :], words[:, first : first + P], ident[:])
+                pairs = flipped[:].rearrange("p (o u) n -> p o n u", u=2)
+                if b == VECTOR_BANK:
+                    nc.vector.tensor_copy(out=grouped_words[:, b], in_=pairs)
+                else:
+                    nc.scalar.copy(out=grouped_words[:, b], in_=pairs)
+            for half in range(2):
+                first = half * (STAGE_CODES // 2)
+                cols = slice(first, first + STAGE_CODES // 2)
+                nc.vector.quantize_mx(
+                    out=codes[:, cols].bitcast(FP8X4),
+                    scales=scales[:, cols],
+                    in_=grouped[:, PACK * first : PACK * (first + STAGE_CODES // 2)],
+                )
+            if i + RESIDENT < STAGES:
+                load_stage(i + RESIDENT)
+            return codes, scales
+
+        def first_product_and_elu(g, codes, scales):
+            a3_sb = a3_pool.tile([P, PACK, WIDTH], F32)
+            grown = elu_pool.tile([P, PACK, WIDTH], F32)
+            for j in range(PACK):
+                sums = sum_psum.tile([P, WIDTH], F32, tag="sums")
+                for c in range(FEATURE_PASSES):
+                    cols = slice((FEATURE_PASSES * j + c) * P, (FEATURE_PASSES * j + c + 1) * P)
+                    nc.tensor.matmul_mx(
+                        out=sums[:],
+                        lhsT=codes[:, cols].bitcast(FP8X4),
+                        lhsT_scale=scales[:, cols],
+                        rhs=w2_codes[:, c].bitcast(FP8X4),
+                        rhs_scale=w2_scales[:, c],
+                        start=(c == 0),
+                        stop=(c == FEATURE_PASSES - 1),
+                    )
+                nc.scalar.activation(out=grown[:, j, :], in_=sums[:], func=ACT.Exp)
+                nc.scalar.copy(out=a3_sb[:, j, :], in_=sums[:])
+            nc.sync.dma_start(
+                out=a3_stage[g], in_=a3_sb[:].rearrange("p (u e) d -> p u e d", e=2)
+            )
+            for u in range(2):
+                nc.vector.tensor_scalar(
+                    out=grown[:, 2 * u : 2 * u + 2, :],
+                    in0=grown[:, 2 * u : 2 * u + 2, :],
+                    scalar1=1.0,
+                    scalar2=-1.0,
+                    op0=ALU.min,
+                    op1=ALU.add,
+                )
+            h_grouped = elu_pool.tile([P, WIDTH, PACK], BF16, align_bytes=64)
+            nc.vector.tensor_tensor(
+                out=h_grouped[:].rearrange("p (x i) t -> p x t i", i=4),
+                in0=a3_sb[:].rearrange("p t (x i) -> p x t i", i=4),
+                in1=grown[:].rearrange("p t (x i) -> p x t i", i=4),
+                op=ALU.max,
+            )
+            nc.vector.quantize_mx(
+                out=h_codes[:, g].bitcast(FP8X4),
+                scales=h_scales[:, g],
+                in_=h_grouped[:].rearrange("p d t -> p (d t)"),
+            )
+
+        def second_product(i, codes, scales):
+            t4_sb = t4_pool.tile([P, A_TILES, WIDTH], F32)
+            sums = [
+                sum_psum.tile([P, WIDTH], F32, name="sums", tag="sums") for r in range(A_TILES)
+            ]
+            for g in range(NODE_GROUPS):
+                for r in range(A_TILES):
+                    cols = slice((NODE_GROUPS * r + g) * P, (NODE_GROUPS * r + g + 1) * P)
+                    nc.tensor.matmul_mx(
+                        out=sums[r][:],
+                        lhsT=codes[:, cols].bitcast(FP8X4),
+                        lhsT_scale=scales[:, cols],
+                        rhs=h_codes[:, g].bitcast(FP8X4),
+                        rhs_scale=h_scales[:, g],
+                        start=(g == 0),
+                        stop=(g == NODE_GROUPS - 1),
+                    )
+            nc.scalar.copy(out=t4_sb[:, 0, :], in_=sums[0][:])
+            nc.vector.tensor_copy(out=t4_sb[:, 1, :], in_=sums[1][:])
+            nc.sync.dma_start(out=t4_stage[i], in_=t4_sb[:])
+
+        operands = {}
+        for i in range(AHEAD):
+            operands[i] = transpose_and_quantise(i)
+        for i in range(STAGES):
+            if i + AHEAD < STAGES:
+                operands[i + AHEAD] = transpose_and_quantise(i + AHEAD)
+            codes, scales = operands[i]
+            if i < T3_STAGES:
+                first_product_and_elu(i, codes, scales)
+            else:
+                second_product(i - T3_STAGES, codes, scales)

@@ -58,7 +58,6 @@ def tile_gcn_kron_pa_kernel(tc, t3, W2, A, out_0, out_1):
         t4_pool = ctx.enter_context(tc.tile_pool(name="t4", bufs=3))
         flip_psum = ctx.enter_context(tc.psum_pool(name="flip", bufs=STAGE_BANKS))
         sum_psum = ctx.enter_context(tc.psum_pool(name="sums", bufs=4))
-        ctx.enter_context(tc.manual_schedule())
 
         rows_of = {}
 

@@ -18,6 +18,8 @@ K_PASS = P * PACK
 NODES = 2048
 FEATURES = 1024
 WIDTH = 512
+HALF = WIDTH // 2
+QUARTER = WIDTH // 4
 
 FEATURE_PASSES = FEATURES // K_PASS
 NODE_GROUPS = NODES // K_PASS
@@ -33,8 +35,9 @@ STAGES = T3_STAGES + A_STAGES
 A_TILES = STAGE_VALUES // NODES
 
 AHEAD = 2
-RESIDENT = 8
-VECTOR_BANK = 3
+LEFT = (0, 1)
+RIGHT = (2, 3)
+VECTOR_BANKS = (2,)
 
 FLOPS = 2 * NODES * FEATURES * WIDTH + 2 * NODES * NODES * WIDTH
 
@@ -50,36 +53,14 @@ def tile_gcn_kron_pa_kernel(tc, t3, W2, A, out_0, out_1):
 
     with ExitStack() as ctx:
         const = ctx.enter_context(tc.tile_pool(name="const", bufs=1))
-        rows_pool = ctx.enter_context(tc.tile_pool(name="rows", bufs=RESIDENT))
-        grouped_pool = ctx.enter_context(tc.tile_pool(name="grouped", bufs=2))
-        codes_pool = ctx.enter_context(tc.tile_pool(name="codes", bufs=AHEAD + 2))
+        rows_pool = ctx.enter_context(tc.tile_pool(name="rows", bufs=10))
+        grouped_pool = ctx.enter_context(tc.tile_pool(name="grouped", bufs=3))
+        codes_pool = ctx.enter_context(tc.tile_pool(name="codes", bufs=STAGES))
         a3_pool = ctx.enter_context(tc.tile_pool(name="a3", bufs=T3_STAGES))
-        elu_pool = ctx.enter_context(tc.tile_pool(name="elu", bufs=2))
-        t4_pool = ctx.enter_context(tc.tile_pool(name="t4", bufs=3))
+        elu_pool = ctx.enter_context(tc.tile_pool(name="elu", bufs=4))
+        t4_pool = ctx.enter_context(tc.tile_pool(name="t4", bufs=4))
         flip_psum = ctx.enter_context(tc.psum_pool(name="flip", bufs=STAGE_BANKS))
         sum_psum = ctx.enter_context(tc.psum_pool(name="sums", bufs=4))
-
-        rows_of = {}
-
-        def load_stage(i):
-            rows = rows_pool.tile([P, STAGE_VALUES], BF16)
-            if i < T3_STAGES:
-                nc.sync.dma_start(
-                    out=rows[:].rearrange("p (u e k) -> p u e k", u=2, e=2), in_=t3_stage[i]
-                )
-            else:
-                nc.sync.dma_start(
-                    out=rows[:].rearrange("p (r m) -> p r m", r=A_TILES), in_=a_stage[i - T3_STAGES]
-                )
-            rows_of[i] = rows
-
-        w2_rows = const.tile([P, FEATURE_PASSES, PACK, WIDTH], BF16)
-        for c in range(FEATURE_PASSES):
-            nc.sync.dma_start(
-                out=w2_rows[:, c].rearrange("p (u e) d -> p u e d", e=2), in_=w2_pass[c]
-            )
-        for i in range(RESIDENT):
-            load_stage(i)
 
         ident = const.tile([P, P], F32)
         make_identity(nc, ident[:])
@@ -89,126 +70,245 @@ def tile_gcn_kron_pa_kernel(tc, t3, W2, A, out_0, out_1):
         nc.vector.memset(zero[:], 0.0)
         nc.scalar.activation(out=one[:], in_=zero[:], func=ACT.Exp)
 
-        w2_grouped = const.tile([P, FEATURE_PASSES, WIDTH, PACK], BF16, align_bytes=64)
         w2_codes = const.tile([P, FEATURE_PASSES, WIDTH], U32, align_bytes=64)
         w2_scales = const.tile([P, FEATURE_PASSES, WIDTH], U8, align_bytes=64)
-        for c in range(FEATURE_PASSES):
-            nc.vector.tensor_copy(
-                out=w2_grouped[:, c].rearrange("p (x i) t -> p x t i", i=4),
-                in_=w2_rows[:, c].rearrange("p t (x i) -> p x t i", i=4),
-            )
-        for c in range(FEATURE_PASSES):
-            nc.vector.quantize_mx(
-                out=w2_codes[:, c].bitcast(FP8X4),
-                scales=w2_scales[:, c],
-                in_=w2_grouped[:, c].rearrange("p d t -> p (d t)"),
-            )
-
         h_codes = const.tile([P, NODE_GROUPS, WIDTH], U32, align_bytes=64)
         h_scales = const.tile([P, NODE_GROUPS, WIDTH], U8, align_bytes=64)
 
-        def transpose_and_quantise(i):
+        ctx.enter_context(tc.manual_schedule())
+
+        w2_rows = rows_pool.tile([P, STAGE_VALUES], BF16, name="rows")
+        w2_view = w2_rows[:].rearrange("p (c t d) -> p c t d", c=FEATURE_PASSES, t=PACK)
+        for c in range(FEATURE_PASSES):
+            nc.sync.dma_start(
+                out=w2_view[:, c].rearrange("p (u e) d -> p u e d", e=2), in_=w2_pass[c]
+            )
+        rows_of = {}
+
+        def load_stage(i):
+            rows = rows_pool.tile([P, STAGE_VALUES], BF16, name="rows")
+            if i == 0:
+                for b in range(STAGE_BANKS):
+                    first = b * FEATURES
+                    nc.sync.dma_start(
+                        out=rows[:, first : first + FEATURES], in_=t3_stage[0][:, b // 2, b % 2, :]
+                    )
+            elif i < T3_STAGES:
+                nc.sync.dma_start(
+                    out=rows[:].rearrange("p (u e k) -> p u e k", u=2, e=2), in_=t3_stage[i]
+                )
+            else:
+                nc.sync.dma_start(
+                    out=rows[:].rearrange("p (r m) -> p r m", r=A_TILES), in_=a_stage[i - T3_STAGES]
+                )
+            rows_of[i] = rows
+
+        for i in range(9):
+            load_stage(i)
+
+        w2_grouped_tile = grouped_pool.tile([P, STAGE_VALUES], BF16, name="grouped", align_bytes=64)
+        w2_grouped = w2_grouped_tile[:].rearrange("p (c d t) -> p c d t", c=FEATURE_PASSES, t=PACK)
+
+        def w2_group(c, half):
+            cols = slice(half * HALF, (half + 1) * HALF)
+            nc.vector.tensor_copy(
+                out=w2_grouped[:, c, cols].rearrange("p (x i) t -> p x t i", i=4),
+                in_=w2_view[:, c, :, cols].rearrange("p t (x i) -> p x t i", i=4),
+            )
+
+        def w2_quantise(c, half):
+            cols = slice(half * HALF, (half + 1) * HALF)
+            nc.vector.quantize_mx(
+                out=w2_codes[:, c, cols].bitcast(FP8X4),
+                scales=w2_scales[:, c, cols],
+                in_=w2_grouped[:, c, cols].rearrange("p d t -> p (d t)"),
+            )
+
+        grouped_of = {}
+        codes_of = {}
+
+        def transpose(i, vector_banks):
             words = rows_of[i][:].bitcast(F32)
-            grouped = grouped_pool.tile([P, STAGE_VALUES], BF16, align_bytes=64)
+            grouped = grouped_pool.tile([P, STAGE_VALUES], BF16, name="grouped", align_bytes=64)
+            grouped_of[i] = grouped
             grouped_words = grouped[:].bitcast(F32).rearrange(
                 "p (b o n u) -> p b o n u", b=STAGE_BANKS, o=2, n=P, u=2
             )
-            codes = codes_pool.tile([P, STAGE_CODES], U32, align_bytes=64)
-            scales = codes_pool.tile([P, STAGE_CODES], U8, align_bytes=64)
             for b in range(STAGE_BANKS):
-                flipped = flip_psum.tile([P, BANK_WORDS // P, P], F32)
+                flipped = flip_psum.tile([P, BANK_WORDS // P, P], F32, name="flipped")
                 for x in range(BANK_WORDS // P):
                     first = b * BANK_WORDS + x * P
                     nc.tensor.transpose(flipped[:, x, :], words[:, first : first + P], ident[:])
                 pairs = flipped[:].rearrange("p (o u) n -> p o n u", u=2)
-                if b == VECTOR_BANK:
+                if b in vector_banks:
                     nc.vector.tensor_copy(out=grouped_words[:, b], in_=pairs)
                 else:
                     nc.scalar.copy(out=grouped_words[:, b], in_=pairs)
-            for half in range(2):
-                first = half * (STAGE_CODES // 2)
-                cols = slice(first, first + STAGE_CODES // 2)
-                nc.vector.quantize_mx(
-                    out=codes[:, cols].bitcast(FP8X4),
-                    scales=scales[:, cols],
-                    in_=grouped[:, PACK * first : PACK * (first + STAGE_CODES // 2)],
-                )
-            if i + RESIDENT < STAGES:
-                load_stage(i + RESIDENT)
-            return codes, scales
 
-        def first_product_and_elu(g, codes, scales):
-            a3_sb = a3_pool.tile([P, PACK, WIDTH], F32)
-            grown = elu_pool.tile([P, PACK, WIDTH], F32)
-            for j in range(PACK):
-                sums = sum_psum.tile([P, WIDTH], F32, tag="sums")
-                for c in range(FEATURE_PASSES):
-                    cols = slice((FEATURE_PASSES * j + c) * P, (FEATURE_PASSES * j + c + 1) * P)
-                    nc.tensor.matmul_mx(
-                        out=sums[:],
-                        lhsT=codes[:, cols].bitcast(FP8X4),
-                        lhsT_scale=scales[:, cols],
-                        rhs=w2_codes[:, c].bitcast(FP8X4),
-                        rhs_scale=w2_scales[:, c],
-                        start=(c == 0),
-                        stop=(c == FEATURE_PASSES - 1),
-                    )
-                nc.scalar.activation(out=grown[:, j, :], in_=sums[:], func=ACT.Exp)
-                nc.scalar.copy(out=a3_sb[:, j, :], in_=sums[:])
-            nc.sync.dma_start(
-                out=a3_stage[g], in_=a3_sb[:].rearrange("p (u e) d -> p u e d", e=2)
-            )
-            for u in range(2):
-                nc.vector.tensor_scalar(
-                    out=grown[:, 2 * u : 2 * u + 2, :],
-                    in0=grown[:, 2 * u : 2 * u + 2, :],
-                    scalar1=1.0,
-                    scalar2=-1.0,
-                    op0=ALU.min,
-                    op1=ALU.add,
-                )
-            h_grouped = elu_pool.tile([P, WIDTH, PACK], BF16, align_bytes=64)
-            nc.vector.tensor_tensor(
-                out=h_grouped[:].rearrange("p (x i) t -> p x t i", i=4),
-                in0=a3_sb[:].rearrange("p t (x i) -> p x t i", i=4),
-                in1=grown[:].rearrange("p t (x i) -> p x t i", i=4),
-                op=ALU.max,
-            )
+        def quantise(i, half):
+            if half == 0:
+                codes = codes_pool.tile([P, STAGE_CODES], U32, name="codes", align_bytes=64)
+                scales = codes_pool.tile([P, STAGE_CODES], U8, name="scales", align_bytes=64)
+                codes_of[i] = codes, scales
+            codes, scales = codes_of[i]
+            first = half * (STAGE_CODES // 2)
+            cols = slice(first, first + STAGE_CODES // 2)
             nc.vector.quantize_mx(
-                out=h_codes[:, g].bitcast(FP8X4),
-                scales=h_scales[:, g],
-                in_=h_grouped[:].rearrange("p d t -> p (d t)"),
+                out=codes[:, cols].bitcast(FP8X4),
+                scales=scales[:, cols],
+                in_=grouped_of[i][:, PACK * first : PACK * (first + STAGE_CODES // 2)],
             )
 
-        def second_product(i, codes, scales):
-            t4_sb = t4_pool.tile([P, A_TILES, WIDTH], F32)
-            sums = [
-                sum_psum.tile([P, WIDTH], F32, name="sums", tag="sums") for r in range(A_TILES)
-            ]
-            for g in range(NODE_GROUPS):
-                for r in range(A_TILES):
+        sums_of = {}
+        a3_of = {}
+        grown_of = {}
+        h_grouped_of = {}
+
+        def first_product(g, quarters):
+            codes, scales = codes_of[g]
+            for q in quarters:
+                sums = sum_psum.tile([P, PACK, QUARTER], F32, name="sums")
+                out_cols = slice(q * QUARTER, (q + 1) * QUARTER)
+                for j in range(PACK):
+                    for c in range(FEATURE_PASSES):
+                        o = FEATURE_PASSES * j + c
+                        cols = slice(o * P, (o + 1) * P)
+                        nc.tensor.matmul_mx(
+                            out=sums[:, j, :],
+                            lhsT=codes[:, cols].bitcast(FP8X4),
+                            lhsT_scale=scales[:, cols],
+                            rhs=w2_codes[:, c, out_cols].bitcast(FP8X4),
+                            rhs_scale=w2_scales[:, c, out_cols],
+                            start=(c == 0),
+                            stop=(c == FEATURE_PASSES - 1),
+                        )
+                sums_of[g, q] = sums
+
+        def leave_psum(g, quarters):
+            if g not in a3_of:
+                a3_of[g] = a3_pool.tile([P, PACK, WIDTH], F32, name="a3")
+            for q in quarters:
+                grown = elu_pool.tile([P, PACK, QUARTER], F32, name="grown")
+                nc.scalar.activation(out=grown[:], in_=sums_of[g, q][:], func=ACT.Exp)
+                grown_of[g, q] = grown
+            for q in quarters:
+                cols = slice(q * QUARTER, (q + 1) * QUARTER)
+                nc.scalar.copy(out=a3_of[g][:, :, cols], in_=sums_of[g, q][:])
+
+        def elu(g, quarters):
+            for q in quarters:
+                grown = grown_of[g, q]
+                nc.vector.tensor_scalar(
+                    out=grown[:], in0=grown[:], scalar1=1.0, scalar2=-1.0, op0=ALU.min, op1=ALU.add
+                )
+            for q in quarters:
+                cols = slice(q * QUARTER, (q + 1) * QUARTER)
+                h_grouped = elu_pool.tile([P, QUARTER, PACK], BF16, name="h_grouped", align_bytes=64)
+                nc.vector.tensor_tensor(
+                    out=h_grouped[:].rearrange("p (x i) t -> p x t i", i=4),
+                    in0=a3_of[g][:, :, cols].rearrange("p t (x i) -> p x t i", i=4),
+                    in1=grown_of[g, q][:].rearrange("p t (x i) -> p x t i", i=4),
+                    op=ALU.max,
+                )
+                h_grouped_of[g, q] = h_grouped
+
+        def quantise_h(g, quarters):
+            for q in quarters:
+                cols = slice(q * QUARTER, (q + 1) * QUARTER)
+                nc.vector.quantize_mx(
+                    out=h_codes[:, g, cols].bitcast(FP8X4),
+                    scales=h_scales[:, g, cols],
+                    in_=h_grouped_of[g, q][:].rearrange("p d t -> p (d t)"),
+                )
+
+        def second_product(i, half):
+            codes, scales = codes_of[T3_STAGES + i]
+            out_cols = slice(half * HALF, (half + 1) * HALF)
+            sums = sum_psum.tile([P, A_TILES, HALF], F32, name="sums")
+            for r in range(A_TILES):
+                for g in range(NODE_GROUPS):
                     cols = slice((NODE_GROUPS * r + g) * P, (NODE_GROUPS * r + g + 1) * P)
                     nc.tensor.matmul_mx(
-                        out=sums[r][:],
+                        out=sums[:, r, :],
                         lhsT=codes[:, cols].bitcast(FP8X4),
                         lhsT_scale=scales[:, cols],
-                        rhs=h_codes[:, g].bitcast(FP8X4),
-                        rhs_scale=h_scales[:, g],
+                        rhs=h_codes[:, g, out_cols].bitcast(FP8X4),
+                        rhs_scale=h_scales[:, g, out_cols],
                         start=(g == 0),
                         stop=(g == NODE_GROUPS - 1),
                     )
-            nc.scalar.copy(out=t4_sb[:, 0, :], in_=sums[0][:])
-            nc.vector.tensor_copy(out=t4_sb[:, 1, :], in_=sums[1][:])
-            nc.sync.dma_start(out=t4_stage[i], in_=t4_sb[:])
+            sums_of["t4", i, half] = sums
 
-        operands = {}
-        for i in range(AHEAD):
-            operands[i] = transpose_and_quantise(i)
-        for i in range(STAGES):
-            if i + AHEAD < STAGES:
-                operands[i + AHEAD] = transpose_and_quantise(i + AHEAD)
-            codes, scales = operands[i]
-            if i < T3_STAGES:
-                first_product_and_elu(i, codes, scales)
+        def store_t4(i, half):
+            t4_sb = t4_pool.tile([P, A_TILES, HALF], F32, name="t4_sb")
+            if (i + half) % 2 == 0:
+                nc.scalar.copy(out=t4_sb[:], in_=sums_of["t4", i, half][:])
             else:
-                second_product(i - T3_STAGES, codes, scales)
+                nc.vector.tensor_copy(out=t4_sb[:], in_=sums_of["t4", i, half][:])
+            nc.sync.dma_start(
+                out=t4_stage[i][:, :, half * HALF : (half + 1) * HALF], in_=t4_sb[:]
+            )
+
+        transpose(0, ())
+        w2_group(0, 0)
+        w2_group(0, 1)
+        w2_group(1, 0)
+        w2_quantise(0, 0)
+        w2_quantise(1, 0)
+        w2_group(1, 1)
+        w2_quantise(0, 1)
+        quantise(0, 0)
+        w2_quantise(1, 1)
+        quantise(0, 1)
+        first_product(0, LEFT)
+
+        for g in range(T3_STAGES):
+            if 9 + g < STAGES:
+                load_stage(9 + g)
+            leave_psum(g, LEFT)
+            elu(g, LEFT)
+            if g == 0:
+                transpose(1, (0, 2))
+                quantise_h(0, LEFT)
+                quantise(1, 0)
+                quantise(1, 1)
+                transpose(2, VECTOR_BANKS)
+                first_product(1, LEFT)
+                quantise(2, 0)
+                quantise(2, 1)
+            else:
+                transpose(g + AHEAD, VECTOR_BANKS)
+                quantise_h(g, LEFT)
+                if g + 1 < T3_STAGES:
+                    first_product(g + 1, LEFT)
+                quantise(g + AHEAD, 0)
+                quantise(g + AHEAD, 1)
+
+        right = 0
+        for i in range(A_STAGES):
+            if i < T3_STAGES:
+                first_product(i, RIGHT)
+            second_product(i, 0)
+            if i < T3_STAGES:
+                leave_psum(i, RIGHT)
+                elu(i, RIGHT)
+            ahead = T3_STAGES + i + AHEAD
+            if ahead < STAGES:
+                transpose(ahead, VECTOR_BANKS)
+            store_t4(i, 0)
+            if i < T3_STAGES:
+                quantise_h(i, RIGHT)
+                nc.sync.dma_start(
+                    out=a3_stage[i], in_=a3_of[i][:].rearrange("p (u e) d -> p u e d", e=2)
+                )
+            if ahead < STAGES:
+                quantise(ahead, 0)
+                quantise(ahead, 1)
+            if i >= T3_STAGES:
+                second_product(right, 1)
+                store_t4(right, 1)
+                right += 1
+        while right < A_STAGES:
+            second_product(right, 1)
+            store_t4(right, 1)
+            right += 1

@@ -70,6 +70,9 @@ def tile_gcn_kron_pa_kernel(tc, t3, W2, A, out_0, out_1):
         nc.vector.memset(zero[:], 0.0)
         nc.scalar.activation(out=one[:], in_=zero[:], func=ACT.Exp)
 
+        zeros = const.tile([P, BANK_WORDS], BF16)
+        nc.gpsimd.memset(zeros[:], 0.0)
+
         w2_codes = const.tile([P, FEATURE_PASSES, WIDTH], U32, align_bytes=64)
         w2_scales = const.tile([P, FEATURE_PASSES, WIDTH], U8, align_bytes=64)
         h_codes = const.tile([P, NODE_GROUPS, WIDTH], U32, align_bytes=64)
@@ -164,10 +167,26 @@ def tile_gcn_kron_pa_kernel(tc, t3, W2, A, out_0, out_1):
         grown_of = {}
         h_grouped_of = {}
 
+        def keep_warm(g, count):
+            q = LEFT[0] if g < T3_STAGES else RIGHT[0]
+            g %= T3_STAGES
+            if (g, q) not in sums_of:
+                sums_of[g, q] = sum_psum.tile([P, PACK, QUARTER], F32, name="sums")
+            for n in range(count):
+                nc.tensor.matmul(
+                    out=sums_of[g, q][:].rearrange("p j n -> p (j n)"),
+                    lhsT=zeros[:, :P],
+                    rhs=zeros[:],
+                    start=True,
+                    stop=True,
+                )
+
         def first_product(g, quarters):
             codes, scales = codes_of[g]
             for q in quarters:
-                sums = sum_psum.tile([P, PACK, QUARTER], F32, name="sums")
+                if (g, q) not in sums_of:
+                    sums_of[g, q] = sum_psum.tile([P, PACK, QUARTER], F32, name="sums")
+                sums = sums_of[g, q]
                 out_cols = slice(q * QUARTER, (q + 1) * QUARTER)
                 for j in range(PACK):
                     for c in range(FEATURE_PASSES):
@@ -182,7 +201,6 @@ def tile_gcn_kron_pa_kernel(tc, t3, W2, A, out_0, out_1):
                             start=(c == 0),
                             stop=(c == FEATURE_PASSES - 1),
                         )
-                sums_of[g, q] = sums
 
         def leave_psum(g, quarters):
             if g not in a3_of:
@@ -260,7 +278,9 @@ def tile_gcn_kron_pa_kernel(tc, t3, W2, A, out_0, out_1):
         quantise(0, 0)
         w2_quantise(1, 1)
         quantise(0, 1)
+        keep_warm(0, 3)
         first_product(0, LEFT)
+        keep_warm(1, 2)
 
         for g in range(T3_STAGES):
             if 9 + g < STAGES:
@@ -272,13 +292,16 @@ def tile_gcn_kron_pa_kernel(tc, t3, W2, A, out_0, out_1):
                 quantise_h(0, LEFT)
                 quantise(1, 0)
                 quantise(1, 1)
+                keep_warm(1, 2)
                 transpose(2, VECTOR_BANKS)
+                keep_warm(1, 2)
                 first_product(1, LEFT)
                 quantise(2, 0)
                 quantise(2, 1)
             else:
                 transpose(g + AHEAD, VECTOR_BANKS)
                 quantise_h(g, LEFT)
+                keep_warm(g + 1, 1)
                 if g + 1 < T3_STAGES:
                     first_product(g + 1, LEFT)
                 quantise(g + AHEAD, 0)

@@ -35,9 +35,9 @@ STAGES = T3_STAGES + A_STAGES
 A_TILES = STAGE_VALUES // NODES
 
 AHEAD = 2
-LEFT = (0, 1)
-RIGHT = (2, 3)
-VECTOR_BANKS = (2,)
+QUARTERS = (0, 1)
+PAIRS = (0, 1)
+RESIDENT = 7
 
 FLOPS = 2 * NODES * FEATURES * WIDTH + 2 * NODES * NODES * WIDTH
 
@@ -53,12 +53,13 @@ def tile_gcn_kron_pa_kernel(tc, t3, W2, A, out_0, out_1):
 
     with ExitStack() as ctx:
         const = ctx.enter_context(tc.tile_pool(name="const", bufs=1))
-        rows_pool = ctx.enter_context(tc.tile_pool(name="rows", bufs=10))
+        rows_pool = ctx.enter_context(tc.tile_pool(name="rows", bufs=RESIDENT + 1))
         grouped_pool = ctx.enter_context(tc.tile_pool(name="grouped", bufs=3))
         codes_pool = ctx.enter_context(tc.tile_pool(name="codes", bufs=STAGES))
         a3_pool = ctx.enter_context(tc.tile_pool(name="a3", bufs=T3_STAGES))
-        elu_pool = ctx.enter_context(tc.tile_pool(name="elu", bufs=4))
-        t4_pool = ctx.enter_context(tc.tile_pool(name="t4", bufs=4))
+        left_pool = ctx.enter_context(tc.tile_pool(name="left", bufs=4))
+        right_pool = ctx.enter_context(tc.tile_pool(name="right", bufs=2))
+        t4_pool = ctx.enter_context(tc.tile_pool(name="t4", bufs=6))
         flip_psum = ctx.enter_context(tc.psum_pool(name="flip", bufs=STAGE_BANKS))
         sum_psum = ctx.enter_context(tc.psum_pool(name="sums", bufs=4))
 
@@ -71,7 +72,7 @@ def tile_gcn_kron_pa_kernel(tc, t3, W2, A, out_0, out_1):
         nc.scalar.activation(out=one[:], in_=zero[:], func=ACT.Exp)
 
         zeros = const.tile([P, BANK_WORDS], BF16)
-        nc.gpsimd.memset(zeros[:], 0.0)
+        nc.vector.memset(zeros[:], 0.0)
 
         w2_codes = const.tile([P, FEATURE_PASSES, WIDTH], U32, align_bytes=64)
         w2_scales = const.tile([P, FEATURE_PASSES, WIDTH], U8, align_bytes=64)
@@ -82,10 +83,15 @@ def tile_gcn_kron_pa_kernel(tc, t3, W2, A, out_0, out_1):
 
         w2_rows = rows_pool.tile([P, STAGE_VALUES], BF16, name="rows")
         w2_view = w2_rows[:].rearrange("p (c t d) -> p c t d", c=FEATURE_PASSES, t=PACK)
-        for c in range(FEATURE_PASSES):
-            nc.sync.dma_start(
-                out=w2_view[:, c].rearrange("p (u e) d -> p u e d", e=2), in_=w2_pass[c]
-            )
+
+        def load_w2(half):
+            cols = slice(half * HALF, (half + 1) * HALF)
+            for c in range(FEATURE_PASSES):
+                for u in range(2):
+                    nc.sync.dma_start(
+                        out=w2_view[:, c, 2 * u : 2 * u + 2, cols], in_=w2_pass[c][:, u, :, cols]
+                    )
+
         rows_of = {}
 
         def load_stage(i):
@@ -106,7 +112,10 @@ def tile_gcn_kron_pa_kernel(tc, t3, W2, A, out_0, out_1):
                 )
             rows_of[i] = rows
 
-        for i in range(9):
+        load_w2(0)
+        load_stage(0)
+        load_w2(1)
+        for i in range(1, RESIDENT):
             load_stage(i)
 
         w2_grouped_tile = grouped_pool.tile([P, STAGE_VALUES], BF16, name="grouped", align_bytes=64)
@@ -168,86 +177,131 @@ def tile_gcn_kron_pa_kernel(tc, t3, W2, A, out_0, out_1):
         h_grouped_of = {}
 
         def keep_warm(g, count):
-            q = LEFT[0] if g < T3_STAGES else RIGHT[0]
-            g %= T3_STAGES
-            if (g, q) not in sums_of:
-                sums_of[g, q] = sum_psum.tile([P, PACK, QUARTER], F32, name="sums")
+            if (g, 0) not in sums_of:
+                sums_of[g, 0] = sum_psum.tile([P, BANK_WORDS], F32, name="sums")
             for n in range(count):
                 nc.tensor.matmul(
-                    out=sums_of[g, q][:].rearrange("p j n -> p (j n)"),
+                    out=sums_of[g, 0][:],
                     lhsT=zeros[:, :P],
                     rhs=zeros[:],
                     start=True,
                     stop=True,
                 )
 
-        def first_product(g, quarters):
+        def first_product_bank(key, g, tiles, out_cols):
+            if key not in sums_of:
+                sums_of[key] = sum_psum.tile([P, BANK_WORDS], F32, name="sums")
+            bank = sums_of[key][:].rearrange("p (j n) -> p j n", j=len(tiles))
             codes, scales = codes_of[g]
-            for q in quarters:
-                if (g, q) not in sums_of:
-                    sums_of[g, q] = sum_psum.tile([P, PACK, QUARTER], F32, name="sums")
-                sums = sums_of[g, q]
-                out_cols = slice(q * QUARTER, (q + 1) * QUARTER)
-                for j in range(PACK):
-                    for c in range(FEATURE_PASSES):
-                        o = FEATURE_PASSES * j + c
-                        cols = slice(o * P, (o + 1) * P)
-                        nc.tensor.matmul_mx(
-                            out=sums[:, j, :],
-                            lhsT=codes[:, cols].bitcast(FP8X4),
-                            lhsT_scale=scales[:, cols],
-                            rhs=w2_codes[:, c, out_cols].bitcast(FP8X4),
-                            rhs_scale=w2_scales[:, c, out_cols],
-                            start=(c == 0),
-                            stop=(c == FEATURE_PASSES - 1),
-                        )
+            for n, j in enumerate(tiles):
+                for c in range(FEATURE_PASSES):
+                    o = FEATURE_PASSES * j + c
+                    cols = slice(o * P, (o + 1) * P)
+                    nc.tensor.matmul_mx(
+                        out=bank[:, n, :],
+                        lhsT=codes[:, cols].bitcast(FP8X4),
+                        lhsT_scale=scales[:, cols],
+                        rhs=w2_codes[:, c, out_cols].bitcast(FP8X4),
+                        rhs_scale=w2_scales[:, c, out_cols],
+                        start=(c == 0),
+                        stop=(c == FEATURE_PASSES - 1),
+                    )
 
-        def leave_psum(g, quarters):
-            if g not in a3_of:
-                a3_of[g] = a3_pool.tile([P, PACK, WIDTH], F32, name="a3")
-            for q in quarters:
-                grown = elu_pool.tile([P, PACK, QUARTER], F32, name="grown")
-                nc.scalar.activation(out=grown[:], in_=sums_of[g, q][:], func=ACT.Exp)
+        def minus_one(grown):
+            nc.vector.tensor_scalar(
+                out=grown[:], in0=grown[:], scalar1=1.0, scalar2=-1.0, op0=ALU.min, op1=ALU.add
+            )
+
+        def round_and_group(h_grouped, a3_cols, grown):
+            nc.vector.tensor_tensor(
+                out=h_grouped[:].rearrange("p (x i) t -> p x t i", i=4),
+                in0=a3_cols.rearrange("p t (x i) -> p x t i", i=4),
+                in1=grown[:].rearrange("p t (x i) -> p x t i", i=4),
+                op=ALU.max,
+            )
+
+        def quantise_h_cols(g, cols, h_grouped):
+            nc.vector.quantize_mx(
+                out=h_codes[:, g, cols].bitcast(FP8X4),
+                scales=h_scales[:, g, cols],
+                in_=h_grouped[:].rearrange("p d t -> p (d t)"),
+            )
+
+        def left_cols(q):
+            return slice(q * QUARTER, (q + 1) * QUARTER)
+
+        def left_product(g):
+            for q in QUARTERS:
+                first_product_bank((g, q), g, range(PACK), left_cols(q))
+
+        def left_elu(g):
+            a3_of[g] = a3_pool.tile([P, PACK, WIDTH], F32, name="a3")
+            for q in QUARTERS:
+                grown = left_pool.tile([P, PACK, QUARTER], F32, name="grown")
                 grown_of[g, q] = grown
-            for q in quarters:
-                cols = slice(q * QUARTER, (q + 1) * QUARTER)
-                nc.scalar.copy(out=a3_of[g][:, :, cols], in_=sums_of[g, q][:])
-
-        def elu(g, quarters):
-            for q in quarters:
-                grown = grown_of[g, q]
-                nc.vector.tensor_scalar(
-                    out=grown[:], in0=grown[:], scalar1=1.0, scalar2=-1.0, op0=ALU.min, op1=ALU.add
+                nc.scalar.activation(
+                    out=grown[:].rearrange("p j n -> p (j n)"), in_=sums_of[g, q][:], func=ACT.Exp
                 )
-            for q in quarters:
-                cols = slice(q * QUARTER, (q + 1) * QUARTER)
-                h_grouped = elu_pool.tile([P, QUARTER, PACK], BF16, name="h_grouped", align_bytes=64)
-                nc.vector.tensor_tensor(
-                    out=h_grouped[:].rearrange("p (x i) t -> p x t i", i=4),
-                    in0=a3_of[g][:, :, cols].rearrange("p t (x i) -> p x t i", i=4),
-                    in1=grown_of[g, q][:].rearrange("p t (x i) -> p x t i", i=4),
-                    op=ALU.max,
+            for q in QUARTERS:
+                nc.scalar.copy(
+                    out=a3_of[g][:, :, left_cols(q)],
+                    in_=sums_of[g, q][:].rearrange("p (j n) -> p j n", j=PACK),
                 )
+            for q in QUARTERS:
+                minus_one(grown_of[g, q])
+            for q in QUARTERS:
+                h_grouped = left_pool.tile([P, QUARTER, PACK], BF16, name="h_grouped", align_bytes=64)
                 h_grouped_of[g, q] = h_grouped
+                round_and_group(h_grouped, a3_of[g][:, :, left_cols(q)], grown_of[g, q])
 
-        def quantise_h(g, quarters):
-            for q in quarters:
-                cols = slice(q * QUARTER, (q + 1) * QUARTER)
-                nc.vector.quantize_mx(
-                    out=h_codes[:, g, cols].bitcast(FP8X4),
-                    scales=h_scales[:, g, cols],
-                    in_=h_grouped_of[g, q][:].rearrange("p d t -> p (d t)"),
+        def left_quantise(g):
+            for q in QUARTERS:
+                quantise_h_cols(g, left_cols(q), h_grouped_of[g, q])
+
+        right_cols = slice(HALF, WIDTH)
+
+        def right_product(g):
+            for pair in PAIRS:
+                tiles = (2 * pair, 2 * pair + 1)
+                first_product_bank((T3_STAGES + g, pair), g, tiles, right_cols)
+
+        def right_exp(g):
+            grown = right_pool.tile([P, PACK, HALF], F32, name="grown_right")
+            grown_of[g] = grown
+            for pair in PAIRS:
+                nc.scalar.activation(
+                    out=grown[:, 2 * pair : 2 * pair + 2, :].rearrange("p j n -> p (j n)"),
+                    in_=sums_of[T3_STAGES + g, pair][:],
+                    func=ACT.Exp,
                 )
+            for pair in PAIRS:
+                nc.scalar.copy(
+                    out=a3_of[g][:, 2 * pair : 2 * pair + 2, right_cols],
+                    in_=sums_of[T3_STAGES + g, pair][:].rearrange("p (j n) -> p j n", j=2),
+                )
+            nc.sync.dma_start(
+                out=a3_stage[g], in_=a3_of[g][:].rearrange("p (u e) d -> p u e d", e=2)
+            )
+            minus_one(grown)
 
-        def second_product(i, half):
+        def right_group(g):
+            h_grouped = right_pool.tile([P, HALF, PACK], BF16, name="h_right", align_bytes=64)
+            h_grouped_of[g] = h_grouped
+            round_and_group(h_grouped, a3_of[g][:, :, right_cols], grown_of[g])
+
+        def right_quantise(g):
+            quantise_h_cols(g, right_cols, h_grouped_of[g])
+
+        def second_product(i, half, tiles=(0, 1)):
             codes, scales = codes_of[T3_STAGES + i]
             out_cols = slice(half * HALF, (half + 1) * HALF)
-            sums = sum_psum.tile([P, A_TILES, HALF], F32, name="sums")
-            for r in range(A_TILES):
+            sums = sum_psum.tile([P, BANK_WORDS], F32, name="sums")
+            bank = sums[:].rearrange("p (r n) -> p r n", n=HALF)
+            for n, r in enumerate(tiles):
                 for g in range(NODE_GROUPS):
                     cols = slice((NODE_GROUPS * r + g) * P, (NODE_GROUPS * r + g + 1) * P)
                     nc.tensor.matmul_mx(
-                        out=sums[:, r, :],
+                        out=bank[:, n, :],
                         lhsT=codes[:, cols].bitcast(FP8X4),
                         lhsT_scale=scales[:, cols],
                         rhs=h_codes[:, g, out_cols].bitcast(FP8X4),
@@ -255,83 +309,84 @@ def tile_gcn_kron_pa_kernel(tc, t3, W2, A, out_0, out_1):
                         start=(g == 0),
                         stop=(g == NODE_GROUPS - 1),
                     )
-            sums_of["t4", i, half] = sums
+            sums_of["t4", i, half] = bank[:, : len(tiles), :]
 
-        def store_t4(i, half):
+        def store_t4(i, half, on_vector, tiles=(0, 1)):
             t4_sb = t4_pool.tile([P, A_TILES, HALF], F32, name="t4_sb")
-            if (i + half) % 2 == 0:
-                nc.scalar.copy(out=t4_sb[:], in_=sums_of["t4", i, half][:])
-            else:
-                nc.vector.tensor_copy(out=t4_sb[:], in_=sums_of["t4", i, half][:])
+            copy = nc.vector.tensor_copy if on_vector else nc.scalar.copy
+            copy(out=t4_sb[:, : len(tiles), :], in_=sums_of["t4", i, half])
             nc.sync.dma_start(
-                out=t4_stage[i][:, :, half * HALF : (half + 1) * HALF], in_=t4_sb[:]
+                out=t4_stage[i][:, tiles[0] : tiles[-1] + 1, half * HALF : (half + 1) * HALF],
+                in_=t4_sb[:, : len(tiles), :],
             )
 
+        keep_warm(0, 6)
         transpose(0, ())
         w2_group(0, 0)
-        w2_group(0, 1)
         w2_group(1, 0)
         w2_quantise(0, 0)
         w2_quantise(1, 0)
-        w2_group(1, 1)
-        w2_quantise(0, 1)
         quantise(0, 0)
-        w2_quantise(1, 1)
         quantise(0, 1)
-        keep_warm(0, 3)
-        first_product(0, LEFT)
+        w2_group(0, 1)
+        w2_group(1, 1)
+        keep_warm(0, 4)
+        left_product(0)
         keep_warm(1, 2)
 
         for g in range(T3_STAGES):
-            if 9 + g < STAGES:
-                load_stage(9 + g)
-            leave_psum(g, LEFT)
-            elu(g, LEFT)
+            left_elu(g)
             if g == 0:
-                transpose(1, (0, 2))
-                quantise_h(0, LEFT)
+                transpose(1, (2,))
+                left_quantise(0)
                 quantise(1, 0)
                 quantise(1, 1)
+                w2_quantise(0, 1)
+                w2_quantise(1, 1)
+                keep_warm(1, 3)
+                load_stage(7)
+                load_stage(8)
+                transpose(2, (2,))
                 keep_warm(1, 2)
-                transpose(2, VECTOR_BANKS)
-                keep_warm(1, 2)
-                first_product(1, LEFT)
+                left_product(1)
                 quantise(2, 0)
                 quantise(2, 1)
             else:
-                transpose(g + AHEAD, VECTOR_BANKS)
-                quantise_h(g, LEFT)
+                load_stage(8 + g)
+                transpose(g + AHEAD, (2,))
+                left_quantise(g)
                 keep_warm(g + 1, 1)
                 if g + 1 < T3_STAGES:
-                    first_product(g + 1, LEFT)
+                    left_product(g + 1)
                 quantise(g + AHEAD, 0)
                 quantise(g + AHEAD, 1)
 
-        right = 0
         for i in range(A_STAGES):
-            if i < T3_STAGES:
-                first_product(i, RIGHT)
-            second_product(i, 0)
-            if i < T3_STAGES:
-                leave_psum(i, RIGHT)
-                elu(i, RIGHT)
             ahead = T3_STAGES + i + AHEAD
-            if ahead < STAGES:
-                transpose(ahead, VECTOR_BANKS)
-            store_t4(i, 0)
             if i < T3_STAGES:
-                quantise_h(i, RIGHT)
-                nc.sync.dma_start(
-                    out=a3_stage[i], in_=a3_of[i][:].rearrange("p (u e) d -> p u e d", e=2)
-                )
+                right_product(i)
+            if i > 0:
+                second_product(i, 0)
+            if i < T3_STAGES:
+                right_exp(i)
+            if ahead < STAGES:
+                transpose(ahead, (0,))
+            if i == 0:
+                second_product(i, 0)
+            if i < T3_STAGES:
+                right_group(i)
+            store_t4(i, 0, on_vector=(i % 2 == 0))
+            if i < T3_STAGES:
+                right_quantise(i)
             if ahead < STAGES:
                 quantise(ahead, 0)
                 quantise(ahead, 1)
             if i >= T3_STAGES:
-                second_product(right, 1)
-                store_t4(right, 1)
-                right += 1
-        while right < A_STAGES:
-            second_product(right, 1)
-            store_t4(right, 1)
-            right += 1
+                second_product(i - T3_STAGES, 1)
+                store_t4(i - T3_STAGES, 1, on_vector=(i % 2 == 0))
+        for i in range(A_STAGES - T3_STAGES, A_STAGES - 1):
+            second_product(i, 1)
+            store_t4(i, 1, on_vector=(i % 2 == 0))
+        for r in range(A_TILES):
+            second_product(A_STAGES - 1, 1, (r,))
+            store_t4(A_STAGES - 1, 1, on_vector=(r == 1), tiles=(r,))

@@ -139,7 +139,7 @@ def tile_gcn_kron_pa_kernel(tc, t3, W2, A, out_0, out_1):
         grouped_of = {}
         codes_of = {}
 
-        def transpose(i, vector_banks):
+        def transpose(i, vector_banks, warm=0):
             words = rows_of[i][:].bitcast(F32)
             grouped = grouped_pool.tile([P, STAGE_VALUES], BF16, name="grouped", align_bytes=64)
             grouped_of[i] = grouped
@@ -151,6 +151,8 @@ def tile_gcn_kron_pa_kernel(tc, t3, W2, A, out_0, out_1):
                 for x in range(BANK_WORDS // P):
                     first = b * BANK_WORDS + x * P
                     nc.tensor.transpose(flipped[:, x, :], words[:, first : first + P], ident[:])
+                if b + 1 < STAGE_BANKS:
+                    keep_warm(0, warm)
                 pairs = flipped[:].rearrange("p (o u) n -> p o n u", u=2)
                 if b in vector_banks:
                     nc.vector.tensor_copy(out=grouped_words[:, b], in_=pairs)
@@ -320,8 +322,8 @@ def tile_gcn_kron_pa_kernel(tc, t3, W2, A, out_0, out_1):
                 in_=t4_sb[:, : len(tiles), :],
             )
 
-        keep_warm(0, 6)
-        transpose(0, ())
+        keep_warm(0, 5)
+        transpose(0, (), warm=1)
         w2_group(0, 0)
         w2_group(1, 0)
         w2_quantise(0, 0)
@@ -330,7 +332,7 @@ def tile_gcn_kron_pa_kernel(tc, t3, W2, A, out_0, out_1):
         quantise(0, 1)
         w2_group(0, 1)
         w2_group(1, 1)
-        keep_warm(0, 4)
+        keep_warm(0, 2)
         left_product(0)
         keep_warm(1, 2)
 
@@ -343,11 +345,11 @@ def tile_gcn_kron_pa_kernel(tc, t3, W2, A, out_0, out_1):
                 quantise(1, 1)
                 w2_quantise(0, 1)
                 w2_quantise(1, 1)
-                keep_warm(1, 3)
+                keep_warm(1, 4)
                 load_stage(7)
                 load_stage(8)
                 transpose(2, (2,))
-                keep_warm(1, 2)
+                keep_warm(1, 1)
                 left_product(1)
                 quantise(2, 0)
                 quantise(2, 1)
@@ -355,7 +357,7 @@ def tile_gcn_kron_pa_kernel(tc, t3, W2, A, out_0, out_1):
                 load_stage(8 + g)
                 transpose(g + AHEAD, (2,))
                 left_quantise(g)
-                keep_warm(g + 1, 1)
+                keep_warm(g + 1, 2 if g + 1 < T3_STAGES else 4)
                 if g + 1 < T3_STAGES:
                     left_product(g + 1)
                 quantise(g + AHEAD, 0)

@@ -74,10 +74,10 @@ def tile_gcn_kron_pa_kernel(tc, t3, W2, A, out_0, out_1):
         zeros = const.tile([P, BANK_WORDS], BF16)
         nc.vector.memset(zeros[:], 0.0)
 
-        w2_codes = const.tile([P, FEATURE_PASSES, WIDTH], U32, align_bytes=64)
-        w2_scales = const.tile([P, FEATURE_PASSES, WIDTH], U8, align_bytes=64)
-        h_codes = const.tile([P, NODE_GROUPS, WIDTH], U32, align_bytes=64)
-        h_scales = const.tile([P, NODE_GROUPS, WIDTH], U8, align_bytes=64)
+        w2_codes = const.tile([P, FEATURE_PASSES, WIDTH], U32, align_bytes=256)
+        w2_scales = const.tile([P, FEATURE_PASSES, WIDTH], U8, align_bytes=256)
+        h_codes = const.tile([P, NODE_GROUPS, WIDTH], U32, align_bytes=256)
+        h_scales = const.tile([P, NODE_GROUPS, WIDTH], U8, align_bytes=256)
 
         ctx.enter_context(tc.manual_schedule())
 
@@ -161,8 +161,8 @@ def tile_gcn_kron_pa_kernel(tc, t3, W2, A, out_0, out_1):
 
         def quantise(i, half):
             if half == 0:
-                codes = codes_pool.tile([P, STAGE_CODES], U32, name="codes", align_bytes=64)
-                scales = codes_pool.tile([P, STAGE_CODES], U8, name="scales", align_bytes=64)
+                codes = codes_pool.tile([P, STAGE_CODES], U32, name="codes", align_bytes=256)
+                scales = codes_pool.tile([P, STAGE_CODES], U8, name="scales", align_bytes=256)
                 codes_of[i] = codes, scales
             codes, scales = codes_of[i]
             first = half * (STAGE_CODES // 2)

from contextlib import ExitStack

import concourse.mybir as mybir
from concourse.masks import make_identity

F32 = mybir.dt.float32
BF16 = mybir.dt.bfloat16
U32 = mybir.dt.uint32
U8 = mybir.dt.uint8
FP8X4 = mybir.dt.float8_e4m3fn_x4
ALU = mybir.AluOpType
ACT = mybir.ActivationFunctionType

P = 128
PACK = 4
K_PASS = P * PACK

NODES = 2048
FEATURES = 1024
WIDTH = 512
HALF = WIDTH // 2
QUARTER = WIDTH // 4

FEATURE_PASSES = FEATURES // K_PASS
NODE_GROUPS = NODES // K_PASS

STAGE_VALUES = 4096
STAGE_WORDS = STAGE_VALUES // 2
STAGE_CODES = STAGE_VALUES // PACK
BANK_WORDS = 512
STAGE_BANKS = STAGE_WORDS // BANK_WORDS
T3_STAGES = NODES * FEATURES // (P * STAGE_VALUES)
A_STAGES = NODES * NODES // (P * STAGE_VALUES)
STAGES = T3_STAGES + A_STAGES
A_TILES = STAGE_VALUES // NODES

AHEAD = 2
QUARTERS = (0, 1)
PAIRS = (0, 1)
RESIDENT = 7

FLOPS = 2 * NODES * FEATURES * WIDTH + 2 * NODES * NODES * WIDTH


def tile_gcn_kron_pa_kernel(tc, t3, W2, A, out_0, out_1):
    nc = tc.nc

    t3_stage = t3.rearrange("(g u p e) k -> g p u e k", g=T3_STAGES, u=2, p=P, e=2)
    a3_stage = out_0.rearrange("(g u p e) d -> g p u e d", g=T3_STAGES, u=2, p=P, e=2)
    a_stage = A.rearrange("(i p r) m -> i p r m", i=A_STAGES, p=P, r=A_TILES)
    t4_stage = out_1.rearrange("(i p r) d -> i p r d", i=A_STAGES, p=P, r=A_TILES)
    w2_pass = W2.rearrange("(c u q e) d -> c q u e d", c=FEATURE_PASSES, u=2, q=P, e=2)

    with ExitStack() as ctx:
        const = ctx.enter_context(tc.tile_pool(name="const", bufs=1))
        rows_pool = ctx.enter_context(tc.tile_pool(name="rows", bufs=RESIDENT + 1))
        grouped_pool = ctx.enter_context(tc.tile_pool(name="grouped", bufs=3))
        codes_pool = ctx.enter_context(tc.tile_pool(name="codes", bufs=STAGES))
        a3_pool = ctx.enter_context(tc.tile_pool(name="a3", bufs=T3_STAGES))
        left_pool = ctx.enter_context(tc.tile_pool(name="left", bufs=4))
        right_pool = ctx.enter_context(tc.tile_pool(name="right", bufs=2))
        t4_pool = ctx.enter_context(tc.tile_pool(name="t4", bufs=6))
        flip_psum = ctx.enter_context(tc.psum_pool(name="flip", bufs=STAGE_BANKS))
        sum_psum = ctx.enter_context(tc.psum_pool(name="sums", bufs=4))

        ident = const.tile([P, P], F32)
        make_identity(nc, ident[:])

        zero = const.tile([P, 1], F32)
        one = const.tile([P, 1], F32)
        nc.vector.memset(zero[:], 0.0)
        nc.scalar.activation(out=one[:], in_=zero[:], func=ACT.Exp)

        zeros = const.tile([P, BANK_WORDS], BF16)
        nc.vector.memset(zeros[:], 0.0)

        w2_codes = const.tile([P, FEATURE_PASSES, WIDTH], U32, align_bytes=256)
        w2_scales = const.tile([P, FEATURE_PASSES, WIDTH], U8, align_bytes=256)
        h_codes = const.tile([P, NODE_GROUPS, WIDTH], U32, align_bytes=256)
        h_scales = const.tile([P, NODE_GROUPS, WIDTH], U8, align_bytes=256)

        ctx.enter_context(tc.manual_schedule())

        w2_rows = rows_pool.tile([P, STAGE_VALUES], BF16, name="rows")
        w2_view = w2_rows[:].rearrange("p (c t d) -> p c t d", c=FEATURE_PASSES, t=PACK)

        def load_w2(half):
            cols = slice(half * HALF, (half + 1) * HALF)
            for c in range(FEATURE_PASSES):
                for u in range(2):
                    nc.sync.dma_start(
                        out=w2_view[:, c, 2 * u : 2 * u + 2, cols], in_=w2_pass[c][:, u, :, cols]
                    )

        rows_of = {}

        def load_stage(i):
            rows = rows_pool.tile([P, STAGE_VALUES], BF16, name="rows")
            if i == 0:
                for b in range(STAGE_BANKS):
                    first = b * FEATURES
                    nc.sync.dma_start(
                        out=rows[:, first : first + FEATURES], in_=t3_stage[0][:, b // 2, b % 2, :]
                    )
            elif i < T3_STAGES:
                nc.sync.dma_start(
                    out=rows[:].rearrange("p (u e k) -> p u e k", u=2, e=2), in_=t3_stage[i]
                )
            else:
                nc.sync.dma_start(
                    out=rows[:].rearrange("p (r m) -> p r m", r=A_TILES), in_=a_stage[i - T3_STAGES]
                )
            rows_of[i] = rows

        load_w2(0)
        load_stage(0)
        load_w2(1)
        for i in range(1, RESIDENT):
            load_stage(i)

        w2_grouped_tile = grouped_pool.tile([P, STAGE_VALUES], BF16, name="grouped", align_bytes=64)
        w2_grouped = w2_grouped_tile[:].rearrange("p (c d t) -> p c d t", c=FEATURE_PASSES, t=PACK)

        def w2_group(c, half):
            cols = slice(half * HALF, (half + 1) * HALF)
            nc.vector.tensor_copy(
                out=w2_grouped[:, c, cols].rearrange("p (x i) t -> p x t i", i=4),
                in_=w2_view[:, c, :, cols].rearrange("p t (x i) -> p x t i", i=4),
            )

        def w2_quantise(c, half):
            cols = slice(half * HALF, (half + 1) * HALF)
            nc.vector.quantize_mx(
                out=w2_codes[:, c, cols].bitcast(FP8X4),
                scales=w2_scales[:, c, cols],
                in_=w2_grouped[:, c, cols].rearrange("p d t -> p (d t)"),
            )

        grouped_of = {}
        codes_of = {}

        def transpose(i, vector_banks, warm=0):
            words = rows_of[i][:].bitcast(F32)
            grouped = grouped_pool.tile([P, STAGE_VALUES], BF16, name="grouped", align_bytes=64)
            grouped_of[i] = grouped
            grouped_words = grouped[:].bitcast(F32).rearrange(
                "p (b o n u) -> p b o n u", b=STAGE_BANKS, o=2, n=P, u=2
            )
            for b in range(STAGE_BANKS):
                flipped = flip_psum.tile([P, BANK_WORDS // P, P], F32, name="flipped")
                for x in range(BANK_WORDS // P):
                    first = b * BANK_WORDS + x * P
                    nc.tensor.transpose(flipped[:, x, :], words[:, first : first + P], ident[:])
                if b + 1 < STAGE_BANKS:
                    keep_warm(0, warm)
                pairs = flipped[:].rearrange("p (o u) n -> p o n u", u=2)
                if b in vector_banks:
                    nc.vector.tensor_copy(out=grouped_words[:, b], in_=pairs)
                else:
                    nc.scalar.copy(out=grouped_words[:, b], in_=pairs)

        def quantise(i, half):
            if half == 0:
                codes = codes_pool.tile([P, STAGE_CODES], U32, name="codes", align_bytes=256)
                scales = codes_pool.tile([P, STAGE_CODES], U8, name="scales", align_bytes=256)
                codes_of[i] = codes, scales
            codes, scales = codes_of[i]
            first = half * (STAGE_CODES // 2)
            cols = slice(first, first + STAGE_CODES // 2)
            nc.vector.quantize_mx(
                out=codes[:, cols].bitcast(FP8X4),
                scales=scales[:, cols],
                in_=grouped_of[i][:, PACK * first : PACK * (first + STAGE_CODES // 2)],
            )

        sums_of = {}
        a3_of = {}
        grown_of = {}
        h_grouped_of = {}

        def keep_warm(g, count):
            if (g, 0) not in sums_of:
                sums_of[g, 0] = sum_psum.tile([P, BANK_WORDS], F32, name="sums")
            for n in range(count):
                nc.tensor.matmul(
                    out=sums_of[g, 0][:],
                    lhsT=zeros[:, :P],
                    rhs=zeros[:],
                    start=True,
                    stop=True,
                )

        def first_product_bank(key, g, tiles, out_cols):
            if key not in sums_of:
                sums_of[key] = sum_psum.tile([P, BANK_WORDS], F32, name="sums")
            bank = sums_of[key][:].rearrange("p (j n) -> p j n", j=len(tiles))
            codes, scales = codes_of[g]
            for n, j in enumerate(tiles):
                for c in range(FEATURE_PASSES):
                    o = FEATURE_PASSES * j + c
                    cols = slice(o * P, (o + 1) * P)
                    nc.tensor.matmul_mx(
                        out=bank[:, n, :],
                        lhsT=codes[:, cols].bitcast(FP8X4),
                        lhsT_scale=scales[:, cols],
                        rhs=w2_codes[:, c, out_cols].bitcast(FP8X4),
                        rhs_scale=w2_scales[:, c, out_cols],
                        start=(c == 0),
                        stop=(c == FEATURE_PASSES - 1),
                    )

        def minus_one(grown):
            nc.vector.tensor_scalar(
                out=grown[:], in0=grown[:], scalar1=1.0, scalar2=-1.0, op0=ALU.min, op1=ALU.add
            )

        def round_and_group(h_grouped, a3_cols, grown):
            nc.vector.tensor_tensor(
                out=h_grouped[:].rearrange("p (x i) t -> p x t i", i=4),
                in0=a3_cols.rearrange("p t (x i) -> p x t i", i=4),
                in1=grown[:].rearrange("p t (x i) -> p x t i", i=4),
                op=ALU.max,
            )

        def quantise_h_cols(g, cols, h_grouped):
            nc.vector.quantize_mx(
                out=h_codes[:, g, cols].bitcast(FP8X4),
                scales=h_scales[:, g, cols],
                in_=h_grouped[:].rearrange("p d t -> p (d t)"),
            )

        def left_cols(q):
            return slice(q * QUARTER, (q + 1) * QUARTER)

        def left_product(g):
            for q in QUARTERS:
                first_product_bank((g, q), g, range(PACK), left_cols(q))

        def left_elu(g):
            a3_of[g] = a3_pool.tile([P, PACK, WIDTH], F32, name="a3")
            for q in QUARTERS:
                grown = left_pool.tile([P, PACK, QUARTER], F32, name="grown")
                grown_of[g, q] = grown
                nc.scalar.activation(
                    out=grown[:].rearrange("p j n -> p (j n)"), in_=sums_of[g, q][:], func=ACT.Exp
                )
            for q in QUARTERS:
                nc.scalar.copy(
                    out=a3_of[g][:, :, left_cols(q)],
                    in_=sums_of[g, q][:].rearrange("p (j n) -> p j n", j=PACK),
                )
            for q in QUARTERS:
                minus_one(grown_of[g, q])
            for q in QUARTERS:
                h_grouped = left_pool.tile([P, QUARTER, PACK], BF16, name="h_grouped", align_bytes=64)
                h_grouped_of[g, q] = h_grouped
                round_and_group(h_grouped, a3_of[g][:, :, left_cols(q)], grown_of[g, q])

        def left_quantise(g):
            for q in QUARTERS:
                quantise_h_cols(g, left_cols(q), h_grouped_of[g, q])

        right_cols = slice(HALF, WIDTH)

        def right_product(g):
            for pair in PAIRS:
                tiles = (2 * pair, 2 * pair + 1)
                first_product_bank((T3_STAGES + g, pair), g, tiles, right_cols)

        def right_exp(g):
            grown = right_pool.tile([P, PACK, HALF], F32, name="grown_right")
            grown_of[g] = grown
            for pair in PAIRS:
                nc.scalar.activation(
                    out=grown[:, 2 * pair : 2 * pair + 2, :].rearrange("p j n -> p (j n)"),
                    in_=sums_of[T3_STAGES + g, pair][:],
                    func=ACT.Exp,
                )
            for pair in PAIRS:
                nc.scalar.copy(
                    out=a3_of[g][:, 2 * pair : 2 * pair + 2, right_cols],
                    in_=sums_of[T3_STAGES + g, pair][:].rearrange("p (j n) -> p j n", j=2),
                )
            nc.sync.dma_start(
                out=a3_stage[g], in_=a3_of[g][:].rearrange("p (u e) d -> p u e d", e=2)
            )
            minus_one(grown)

        def right_group(g):
            h_grouped = right_pool.tile([P, HALF, PACK], BF16, name="h_right", align_bytes=64)
            h_grouped_of[g] = h_grouped
            round_and_group(h_grouped, a3_of[g][:, :, right_cols], grown_of[g])

        def right_quantise(g):
            quantise_h_cols(g, right_cols, h_grouped_of[g])

        def second_product(i, half, tiles=(0, 1)):
            codes, scales = codes_of[T3_STAGES + i]
            out_cols = slice(half * HALF, (half + 1) * HALF)
            sums = sum_psum.tile([P, BANK_WORDS], F32, name="sums")
            bank = sums[:].rearrange("p (r n) -> p r n", n=HALF)
            for n, r in enumerate(tiles):
                for g in range(NODE_GROUPS):
                    cols = slice((NODE_GROUPS * r + g) * P, (NODE_GROUPS * r + g + 1) * P)
                    nc.tensor.matmul_mx(
                        out=bank[:, n, :],
                        lhsT=codes[:, cols].bitcast(FP8X4),
                        lhsT_scale=scales[:, cols],
                        rhs=h_codes[:, g, out_cols].bitcast(FP8X4),
                        rhs_scale=h_scales[:, g, out_cols],
                        start=(g == 0),
                        stop=(g == NODE_GROUPS - 1),
                    )
            sums_of["t4", i, half] = bank[:, : len(tiles), :]

        def store_t4(i, half, on_vector, tiles=(0, 1)):
            t4_sb = t4_pool.tile([P, A_TILES, HALF], F32, name="t4_sb")
            copy = nc.vector.tensor_copy if on_vector else nc.scalar.copy
            copy(out=t4_sb[:, : len(tiles), :], in_=sums_of["t4", i, half])
            nc.sync.dma_start(
                out=t4_stage[i][:, tiles[0] : tiles[-1] + 1, half * HALF : (half + 1) * HALF],
                in_=t4_sb[:, : len(tiles), :],
            )

        keep_warm(0, 5)
        transpose(0, (), warm=1)
        w2_group(0, 0)
        w2_group(1, 0)
        w2_quantise(0, 0)
        w2_quantise(1, 0)
        quantise(0, 0)
        quantise(0, 1)
        w2_group(0, 1)
        w2_group(1, 1)
        keep_warm(0, 2)
        left_product(0)
        keep_warm(1, 2)

        for g in range(T3_STAGES):
            left_elu(g)
            if g == 0:
                transpose(1, (2,))
                left_quantise(0)
                quantise(1, 0)
                quantise(1, 1)
                w2_quantise(0, 1)
                w2_quantise(1, 1)
                keep_warm(1, 4)
                load_stage(7)
                load_stage(8)
                transpose(2, (2,))
                keep_warm(1, 1)
                left_product(1)
                quantise(2, 0)
                quantise(2, 1)
            else:
                load_stage(8 + g)
                transpose(g + AHEAD, (2,))
                left_quantise(g)
                keep_warm(g + 1, 2 if g + 1 < T3_STAGES else 4)
                if g + 1 < T3_STAGES:
                    left_product(g + 1)
                quantise(g + AHEAD, 0)
                quantise(g + AHEAD, 1)

        for i in range(A_STAGES):
            ahead = T3_STAGES + i + AHEAD
            if i < T3_STAGES:
                right_product(i)
            if i > 0:
                second_product(i, 0)
            if i < T3_STAGES:
                right_exp(i)
            if ahead < STAGES:
                transpose(ahead, (0,))
            if i == 0:
                second_product(i, 0)
            if i < T3_STAGES:
                right_group(i)
            store_t4(i, 0, on_vector=(i % 2 == 0))
            if i < T3_STAGES:
                right_quantise(i)
            if ahead < STAGES:
                quantise(ahead, 0)
                quantise(ahead, 1)
            if i >= T3_STAGES:
                second_product(i - T3_STAGES, 1)
                store_t4(i - T3_STAGES, 1, on_vector=(i % 2 == 0))
        for i in range(A_STAGES - T3_STAGES, A_STAGES - 1):
            second_product(i, 1)
            store_t4(i, 1, on_vector=(i % 2 == 0))
        for r in range(A_TILES):
            second_product(A_STAGES - 1, 1, (r,))
            store_t4(A_STAGES - 1, 1, on_vector=(r == 1), tiles=(r,))
